import numpy as np
import ml_dtypes


def mxq(x, axis, fmt="e4m3"):
    dtype, down = {"e4m3": (ml_dtypes.float8_e4m3fn, 7), "e5m2": (ml_dtypes.float8_e5m2, 14)}[fmt]
    v = np.moveaxis(np.asarray(x, np.float32).astype(ml_dtypes.bfloat16).astype(np.float64), axis, -1)
    blocks = v.reshape(v.shape[:-1] + (-1, 32))
    amax = np.abs(blocks).max(-1, keepdims=True)
    byte = np.maximum(np.where(amax > 0, np.frexp(amax)[1] - 1 + 127, 0) - down, 1)
    scale = np.exp2(byte - 127.0)
    codes = (blocks / scale).astype(np.float32).astype(dtype).astype(np.float64)
    return np.moveaxis((codes * scale).reshape(v.shape), -1, axis)


WIDE = False


def mx_kscale(k):
    if not WIDE:
        return np.ones(k)
    levels = np.array([20, -20, 10, -10, 0])
    a = np.random.permutation(np.resize(levels, k // 512 * 4)).reshape(k // 512, 4)
    idx = np.arange(k)
    return np.exp2(a[idx // 512, idx % 128 // 32])


BF16 = ml_dtypes.bfloat16


def bf(x):
    return np.asarray(x, np.float32).astype(BF16)


def f64(x):
    return np.asarray(x).astype(np.float64)


N, CI, CO, H, W, KH, KW = 4, 256, 8192, 10, 9, 3, 2
HO, WO = H - KH + 1, W - KW + 1
L = N * HO * WO


def setup_inputs():
    s = mx_kscale(CO)
    x = np.random.standard_normal((N, CI, H, W))
    y = np.random.standard_normal((N, CO, HO, WO)) / np.sqrt(L) / s[None, :, None, None]
    g = np.random.standard_normal((CO, CI, KH, KW)) * np.exp2(np.random.randint(-12, 1, (1, CI, 1, 1))) * s[:, None, None, None]
    return {"input": bf(x), "grad_output": bf(y), "grad_out": bf(g)}


def reference(input, grad_output, grad_out):
    yq = mxq(f64(grad_output).transpose(1, 0, 2, 3).reshape(CO, L), 0, "e4m3")
    gq = mxq(f64(grad_out).reshape(CO, CI * KH * KW), 0, "e5m2").reshape(CO, CI, KH, KW)
    gx = np.zeros((N, CI, H, W))
    for i in range(KH):
        for j in range(KW):
            t = gq[:, :, i, j].T @ yq
            gx[:, :, i:i + HO, j:j + WO] += t.reshape(CI, N, HO, WO).transpose(1, 0, 2, 3)
    return gx

@@ -1,0 +1,170 @@
+from contextlib import ExitStack
+
+import concourse.mybir as mybir
+from concourse.masks import make_identity
+
+BF16 = mybir.dt.bfloat16
+F32 = mybir.dt.float32
+U32 = mybir.dt.uint32
+U8 = mybir.dt.uint8
+E4M3X4 = mybir.dt.float8_e4m3fn_x4
+E5M2X4 = mybir.dt.float8_e5m2_x4
+
+IMAGES, CI, CO = 4, 256, 8192
+H, W, KH, KW = 10, 9, 3, 2
+HO, WO = H - KH + 1, W - KW + 1
+TAPS = KH * KW
+PLACES = HO * WO
+L = IMAGES * PLACES
+COLS = CI * TAPS
+
+P = 128
+PACK = 4
+K_PASS = P * PACK
+PASSES = CO // K_PASS
+BANK = 512
+RUN = 4
+
+WINDOW_C = 64
+WINDOW_COLS = WINDOW_C * TAPS
+WINDOWS = CI // WINDOW_C
+L_HALVES = L // P
+C_HALVES = CI // P
+WINDOWS_PER_HALF = WINDOWS // C_HALVES
+
+VECTOR_COLS = 640
+
+FLOPS = 2 * CO * COLS * L
+
+
+def regroup(copy, grouped, raw):
+    copy(
+        out=grouped.rearrange("p (q i) j -> p q j i", i=RUN),
+        in_=raw.rearrange("p j (q i) -> p q j i", i=RUN),
+    )
+
+
+def tile_model_pa_k_kernel(tc, image, grad_output, grad_out, out):
+    nc = tc.nc
+    g_rows = grad_out.rearrange("(k p j) c kh kw -> k p j (c kh kw)", p=P, j=PACK)
+    y_rows = grad_output.rearrange("n (k p j) h w -> k p n j (h w)", p=P, j=PACK)
+    out_rows = out.rearrange("n c p q -> c n (p q)")
+
+    with ExitStack() as ctx:
+        const = ctx.enter_context(tc.tile_pool(name="const", bufs=1))
+        raw_pool = ctx.enter_context(tc.tile_pool(name="raw", bufs=6))
+        grouped_pool = ctx.enter_context(tc.tile_pool(name="grouped", bufs=3))
+        mx_pool = ctx.enter_context(tc.tile_pool(name="mx", bufs=3))
+        psum = ctx.enter_context(tc.psum_pool(name="psum", bufs=1))
+
+        ident = const.tile([P, P], F32)
+        make_identity(nc, ident[:])
+        zeros = const.tile([P, BANK], BF16)
+        nc.vector.memset(zeros[:], 0.0)
+        out_sb = [const.tile([P, IMAGES, H, W], F32, name="out_sb%d" % h) for h in range(C_HALVES)]
+        for h in range(C_HALVES):
+            nc.vector.memset(out_sb[h][:], 0.0)
+        t_sb = [const.tile([P, TAPS, CI], F32, name="t_sb%d" % lh) for lh in range(L_HALVES)]
+
+        t_acc = {}
+        for lh in range(L_HALVES):
+            for s in range(WINDOWS):
+                t_acc[lh, s] = psum.tile([P, BANK], F32, name="t_%d_%d" % (lh, s))
+
+        grouped = {}
+
+        def load_and_regroup(k):
+            y_raw = raw_pool.tile([P, IMAGES, PACK, PLACES], BF16)
+            nc.sync.dma_start(out=y_raw[:], in_=y_rows[k])
+            g_raw = raw_pool.tile([P, PACK, COLS], BF16)
+            nc.sync.dma_start(out=g_raw[:], in_=g_rows[k])
+            y_grouped = grouped_pool.tile([P, L, PACK], BF16, align_bytes=64)
+            g_grouped = grouped_pool.tile([P, COLS, PACK], BF16, align_bytes=64)
+            nc.vector.tensor_copy(
+                out=y_grouped[:].rearrange("p (n q i) j -> p n q j i", n=IMAGES, i=RUN),
+                in_=y_raw[:].rearrange("p n j (q i) -> p n q j i", i=RUN),
+            )
+            regroup(nc.vector.tensor_copy, g_grouped[:, :VECTOR_COLS, :], g_raw[:, :, :VECTOR_COLS])
+            regroup(nc.scalar.copy, g_grouped[:, VECTOR_COLS:, :], g_raw[:, :, VECTOR_COLS:])
+            grouped[k] = (y_grouped, g_grouped)
+
+        def quantise_and_multiply(k):
+            y_grouped, g_grouped = grouped.pop(k)
+            y_codes = mx_pool.tile([P, L], U32, align_bytes=64)
+            y_scales = mx_pool.tile([P, L], U8, align_bytes=64)
+            g_codes = mx_pool.tile([P, COLS], U32, align_bytes=64)
+            g_scales = mx_pool.tile([P, COLS], U8, align_bytes=64)
+            nc.vector.quantize_mx(
+                out=y_codes[:].bitcast(E4M3X4),
+                scales=y_scales[:],
+                in_=y_grouped[:].rearrange("p l j -> p (l j)"),
+            )
+            for w0 in range(0, COLS, BANK):
+                nc.vector.quantize_mx(
+                    out=g_codes[:, w0 : w0 + BANK].bitcast(E5M2X4),
+                    scales=g_scales[:, w0 : w0 + BANK],
+                    in_=g_grouped[:, w0 : w0 + BANK, :].rearrange("p w j -> p (w j)"),
+                )
+            for h in range(C_HALVES):
+                for lh in range(L_HALVES):
+                    places = slice(lh * P, (lh + 1) * P)
+                    for s in range(h * WINDOWS_PER_HALF, (h + 1) * WINDOWS_PER_HALF):
+                        w0 = min(s * WINDOW_COLS, COLS - BANK)
+                        nc.tensor.matmul_mx(
+                            out=t_acc[lh, s][:],
+                            lhsT=y_codes[:, places].bitcast(E4M3X4),
+                            lhsT_scale=y_scales[:, places],
+                            rhs=g_codes[:, w0 : w0 + BANK].bitcast(E5M2X4),
+                            rhs_scale=g_scales[:, w0 : w0 + BANK],
+                            start=(k == 0),
+                            stop=(k == PASSES - 1),
+                        )
+
+        for k in range(PASSES + 1):
+            if k < PASSES:
+                load_and_regroup(k)
+            if k > 0:
+                quantise_and_multiply(k - 1)
+
+        copies = [nc.vector.tensor_copy, nc.scalar.copy]
+        for s in range(WINDOWS):
+            first = s * WINDOW_COLS - min(s * WINDOW_COLS, COLS - BANK)
+            for lh in range(L_HALVES):
+                copies[lh](
+                    out=t_sb[lh][:, :, s * WINDOW_C : (s + 1) * WINDOW_C],
+                    in_=t_acc[lh, s][:, first : first + WINDOW_COLS].rearrange(
+                        "p (c t) -> p t c", t=TAPS
+                    ),
+                )
+
+        for h in range(C_HALVES):
+            channels = slice(h * P, (h + 1) * P)
+            sums = {}
+            for kw in reversed(range(KW)):
+                bank = psum.tile([P, BANK], F32, name="sums_%d_%d" % (h, kw), tag="t_%d_%d" % (kw, h))
+                nc.tensor.matmul(out=bank[:], lhsT=zeros[:, :P], rhs=zeros[:], start=True, stop=False)
+                rows = bank[:, : IMAGES * H * WO].rearrange("c (n r) -> c n r", n=IMAGES)
+                for lh in range(L_HALVES):
+                    images = slice(lh * P // PLACES, (lh + 1) * P // PLACES)
+                    for kh in range(KH):
+                        nc.tensor.matmul(
+                            out=rows[:, images, kh * WO : kh * WO + PLACES],
+                            lhsT=t_sb[lh][:, kh * KW + kw, channels],
+                            rhs=ident[:],
+                            is_transpose=True,
+                            start=False,
+                            stop=(lh == L_HALVES - 1 and kh == KH - 1),
+                        )
+                sums[kw] = bank[:, : IMAGES * H * WO].rearrange(
+                    "c (n p j) -> c n p j", n=IMAGES, p=H
+                )
+            nc.scalar.copy(out=out_sb[h][:, :, :, 1 : 1 + WO], in_=sums[1])
+            nc.vector.tensor_tensor(
+                out=out_sb[h][:, :, :, 0:WO],
+                in0=out_sb[h][:, :, :, 0:WO],
+                in1=sums[0],
+                op=mybir.AluOpType.add,
+            )
+            nc.sync.dma_start(
+                out=out_rows[channels], in_=out_sb[h][:].rearrange("c n p q -> c n (p q)")
+            )

@@ -25,16 +25,32 @@ PASSES = CO // K_PASS
 BANK = 512
 RUN = 4
 
-WINDOW_C = 64
-WINDOW_COLS = WINDOW_C * TAPS
-WINDOWS = CI // WINDOW_C
 L_HALVES = L // P
 C_HALVES = CI // P
-WINDOWS_PER_HALF = WINDOWS // C_HALVES
+HALF_COLS = COLS // C_HALVES
 
-VECTOR_COLS = 640
+WINDOW_C = 64
+WINDOW_COLS = WINDOW_C * TAPS
+WINDOWS_PER_HALF = P // WINDOW_C
+WINDOWS = C_HALVES * WINDOWS_PER_HALF
+
+VECTOR_SHARE = (5, 12)
 
 FLOPS = 2 * CO * COLS * L
+
+
+def units():
+    quarter = HALF_COLS // 2
+    plan = [
+        (0, 0, HALF_COLS, [(0, quarter), (quarter, HALF_COLS)], True),
+        (0, HALF_COLS, HALF_COLS, [(HALF_COLS, COLS)], False),
+    ]
+    for k in range(1, PASSES - 2):
+        plan.append((k, 0, COLS, [(0, COLS)], True))
+    for h in range(C_HALVES):
+        for k in (PASSES - 2, PASSES - 1):
+            plan.append((k, h * HALF_COLS, HALF_COLS, [(h * HALF_COLS, (h + 1) * HALF_COLS)], h == 0))
+    return plan
 
 
 def regroup(copy, grouped, raw):
@@ -71,47 +87,78 @@ def tile_model_pa_k_kernel(tc, image, grad_output, grad_out, out):
             for s in range(WINDOWS):
                 t_acc[lh, s] = psum.tile([P, BANK], F32, name="t_%d_%d" % (lh, s))
 
-        grouped = {}
+        y_grouped_of = {}
+        g_grouped_of = {}
+        y_mx_of = {}
 
-        def load_and_regroup(k):
-            y_raw = raw_pool.tile([P, IMAGES, PACK, PLACES], BF16)
-            nc.sync.dma_start(out=y_raw[:], in_=y_rows[k])
-            g_raw = raw_pool.tile([P, PACK, COLS], BF16)
-            nc.sync.dma_start(out=g_raw[:], in_=g_rows[k])
-            y_grouped = grouped_pool.tile([P, L, PACK], BF16, align_bytes=64)
-            g_grouped = grouped_pool.tile([P, COLS, PACK], BF16, align_bytes=64)
-            nc.vector.tensor_copy(
-                out=y_grouped[:].rearrange("p (n q i) j -> p n q j i", n=IMAGES, i=RUN),
-                in_=y_raw[:].rearrange("p n j (q i) -> p n q j i", i=RUN),
-            )
-            regroup(nc.vector.tensor_copy, g_grouped[:, :VECTOR_COLS, :], g_raw[:, :, :VECTOR_COLS])
-            regroup(nc.scalar.copy, g_grouped[:, VECTOR_COLS:, :], g_raw[:, :, VECTOR_COLS:])
-            grouped[k] = (y_grouped, g_grouped)
+        def load_and_regroup(unit):
+            k, col0, ncols, loads, with_y = unit
+            g_grouped = grouped_pool.tile([P, ncols, PACK], BF16, align_bytes=64, name="g_grouped")
+            g_grouped_of[k, col0] = g_grouped
+            raws = []
+            y_raw = None
+            for a, b in loads:
+                if with_y and y_raw is None and (k > 0 or raws):
+                    y_raw = raw_pool.tile([P, IMAGES, PACK, PLACES], BF16, name="y_raw")
+                    nc.sync.dma_start(out=y_raw[:], in_=y_rows[k])
+                g_raw = raw_pool.tile([P, PACK, b - a], BF16, name="g_raw")
+                nc.sync.dma_start(out=g_raw[:], in_=g_rows[k][:, :, a:b])
+                raws.append(g_raw)
 
-        def quantise_and_multiply(k):
-            y_grouped, g_grouped = grouped.pop(k)
-            y_codes = mx_pool.tile([P, L], U32, align_bytes=64)
-            y_scales = mx_pool.tile([P, L], U8, align_bytes=64)
-            g_codes = mx_pool.tile([P, COLS], U32, align_bytes=64)
-            g_scales = mx_pool.tile([P, COLS], U8, align_bytes=64)
-            nc.vector.quantize_mx(
-                out=y_codes[:].bitcast(E4M3X4),
-                scales=y_scales[:],
-                in_=y_grouped[:].rearrange("p l j -> p (l j)"),
-            )
-            for w0 in range(0, COLS, BANK):
+            def regroup_y():
+                y_grouped = grouped_pool.tile([P, L, PACK], BF16, align_bytes=64, name="y_grouped")
+                y_grouped_of[k] = y_grouped
+                nc.vector.tensor_copy(
+                    out=y_grouped[:].rearrange("p (n q i) j -> p n q j i", n=IMAGES, i=RUN),
+                    in_=y_raw[:].rearrange("p n j (q i) -> p n q j i", i=RUN),
+                )
+
+            if with_y and k > 0:
+                regroup_y()
+            for number, (a, b) in enumerate(loads):
+                g_raw = raws[number]
+                split = (b - a) * VECTOR_SHARE[0] // VECTOR_SHARE[1]
+                regroup(
+                    nc.vector.tensor_copy,
+                    g_grouped[:, a - col0 : a - col0 + split, :],
+                    g_raw[:, :, :split],
+                )
+                regroup(nc.scalar.copy, g_grouped[:, a - col0 + split : b - col0, :], g_raw[:, :, split:])
+                if with_y and k == 0 and number == 0:
+                    regroup_y()
+
+        def quantise_and_multiply(unit):
+            k, col0, ncols, loads, with_y = unit
+            if with_y:
+                y_grouped = y_grouped_of.pop(k)
+                y_codes = mx_pool.tile([P, L], U32, align_bytes=64, name="y_codes")
+                y_scales = mx_pool.tile([P, L], U8, align_bytes=64, name="y_scales")
+                y_mx_of[k] = (y_codes, y_scales)
                 nc.vector.quantize_mx(
-                    out=g_codes[:, w0 : w0 + BANK].bitcast(E5M2X4),
-                    scales=g_scales[:, w0 : w0 + BANK],
-                    in_=g_grouped[:, w0 : w0 + BANK, :].rearrange("p w j -> p (w j)"),
+                    out=y_codes[:].bitcast(E4M3X4),
+                    scales=y_scales[:],
+                    in_=y_grouped[:].rearrange("p l j -> p (l j)"),
+                )
+            y_codes, y_scales = y_mx_of[k]
+            g_grouped = g_grouped_of.pop((k, col0))
+            g_codes = mx_pool.tile([P, ncols], U32, align_bytes=64, name="g_codes")
+            g_scales = mx_pool.tile([P, ncols], U8, align_bytes=64, name="g_scales")
+            for w0 in range(0, ncols, BANK):
+                w1 = min(w0 + BANK, ncols)
+                nc.vector.quantize_mx(
+                    out=g_codes[:, w0:w1].bitcast(E5M2X4),
+                    scales=g_scales[:, w0:w1],
+                    in_=g_grouped[:, w0:w1, :].rearrange("p w j -> p (w j)"),
                 )
             for h in range(C_HALVES):
+                if not col0 <= h * HALF_COLS < col0 + ncols:
+                    continue
                 for lh in range(L_HALVES):
                     places = slice(lh * P, (lh + 1) * P)
-                    for s in range(h * WINDOWS_PER_HALF, (h + 1) * WINDOWS_PER_HALF):
-                        w0 = min(s * WINDOW_COLS, COLS - BANK)
+                    for number in range(WINDOWS_PER_HALF):
+                        w0 = h * HALF_COLS - col0 + number * (HALF_COLS - BANK)
                         nc.tensor.matmul_mx(
-                            out=t_acc[lh, s][:],
+                            out=t_acc[lh, h * WINDOWS_PER_HALF + number][:],
                             lhsT=y_codes[:, places].bitcast(E4M3X4),
                             lhsT_scale=y_scales[:, places],
                             rhs=g_codes[:, w0 : w0 + BANK].bitcast(E5M2X4),
@@ -120,24 +167,20 @@ def tile_model_pa_k_kernel(tc, image, grad_output, grad_out, out):
                             stop=(k == PASSES - 1),
                         )
 
-        for k in range(PASSES + 1):
-            if k < PASSES:
-                load_and_regroup(k)
-            if k > 0:
-                quantise_and_multiply(k - 1)
+        def empty_banks(h):
+            copies = [nc.vector.tensor_copy, nc.scalar.copy]
+            for number in range(WINDOWS_PER_HALF):
+                s = h * WINDOWS_PER_HALF + number
+                first = number * (WINDOW_COLS - (HALF_COLS - BANK))
+                for lh in range(L_HALVES):
+                    copies[lh](
+                        out=t_sb[lh][:, :, s * WINDOW_C : (s + 1) * WINDOW_C],
+                        in_=t_acc[lh, s][:, first : first + WINDOW_COLS].rearrange(
+                            "p (c t) -> p t c", t=TAPS
+                        ),
+                    )
 
-        copies = [nc.vector.tensor_copy, nc.scalar.copy]
-        for s in range(WINDOWS):
-            first = s * WINDOW_COLS - min(s * WINDOW_COLS, COLS - BANK)
-            for lh in range(L_HALVES):
-                copies[lh](
-                    out=t_sb[lh][:, :, s * WINDOW_C : (s + 1) * WINDOW_C],
-                    in_=t_acc[lh, s][:, first : first + WINDOW_COLS].rearrange(
-                        "p (c t) -> p t c", t=TAPS
-                    ),
-                )
-
-        for h in range(C_HALVES):
+        def transpose_and_store(h):
             channels = slice(h * P, (h + 1) * P)
             sums = {}
             for kw in reversed(range(KW)):
@@ -168,3 +211,15 @@ def tile_model_pa_k_kernel(tc, image, grad_output, grad_out, out):
             nc.sync.dma_start(
                 out=out_rows[channels], in_=out_sb[h][:].rearrange("c n p q -> c n (p q)")
             )
+
+        plan = units()
+        for i in range(len(plan) + 1):
+            if i < len(plan):
+                load_and_regroup(plan[i])
+            if i == len(plan) - 1:
+                empty_banks(0)
+                transpose_and_store(0)
+            if i > 0:
+                quantise_and_multiply(plan[i - 1])
+        empty_banks(1)
+        transpose_and_store(1)

@@ -27,29 +27,25 @@ RUN = 4
 
 L_HALVES = L // P
 C_HALVES = CI // P
-HALF_COLS = COLS // C_HALVES
 
-WINDOW_C = 64
-WINDOW_COLS = WINDOW_C * TAPS
-WINDOWS_PER_HALF = P // WINDOW_C
-WINDOWS = C_HALVES * WINDOWS_PER_HALF
+WINDOWS = COLS // BANK
 
-VECTOR_SHARE = (5, 12)
+VECTOR_SHARE = (49, 96)
+SHARE_STEP = 2 * RUN
 
 FLOPS = 2 * CO * COLS * L
 
 
 def units():
-    quarter = HALF_COLS // 2
     plan = [
-        (0, 0, HALF_COLS, [(0, quarter), (quarter, HALF_COLS)], True),
-        (0, HALF_COLS, HALF_COLS, [(HALF_COLS, COLS)], False),
+        (0, 0, BANK, [(0, BANK // 2), (BANK // 2, BANK)], True),
+        (0, BANK, COLS - BANK, [(BANK, COLS)], False),
     ]
     for k in range(1, PASSES - 2):
         plan.append((k, 0, COLS, [(0, COLS)], True))
-    for h in range(C_HALVES):
+    for w in range(WINDOWS):
         for k in (PASSES - 2, PASSES - 1):
-            plan.append((k, h * HALF_COLS, HALF_COLS, [(h * HALF_COLS, (h + 1) * HALF_COLS)], h == 0))
+            plan.append((k, w * BANK, BANK, [(w * BANK, (w + 1) * BANK)], w == 0))
     return plan
 
 
@@ -72,9 +68,12 @@ def tile_model_pa_k_kernel(tc, image, grad_output, grad_out, out):
         grouped_pool = ctx.enter_context(tc.tile_pool(name="grouped", bufs=3))
         mx_pool = ctx.enter_context(tc.tile_pool(name="mx", bufs=3))
         psum = ctx.enter_context(tc.psum_pool(name="psum", bufs=1))
+        stage = ctx.enter_context(tc.psum_pool(name="stage", bufs=2))
 
         ident = const.tile([P, P], F32)
         make_identity(nc, ident[:])
+        ident_bf = const.tile([P, P], BF16)
+        make_identity(nc, ident_bf[:])
         zeros = const.tile([P, BANK], BF16)
         nc.vector.memset(zeros[:], 0.0)
         out_sb = [const.tile([P, IMAGES, H, W], F32, name="out_sb%d" % h) for h in range(C_HALVES)]
@@ -108,16 +107,23 @@ def tile_model_pa_k_kernel(tc, image, grad_output, grad_out, out):
             def regroup_y():
                 y_grouped = grouped_pool.tile([P, L, PACK], BF16, align_bytes=64, name="y_grouped")
                 y_grouped_of[k] = y_grouped
-                nc.vector.tensor_copy(
-                    out=y_grouped[:].rearrange("p (n q i) j -> p n q j i", n=IMAGES, i=RUN),
-                    in_=y_raw[:].rearrange("p n j (q i) -> p n q j i", i=RUN),
-                )
+                y_bank = stage.tile([P, L * PACK], BF16, name="y_bank")
+                for lh in range(L_HALVES):
+                    images = slice(lh * P // PLACES, (lh + 1) * P // PLACES)
+                    nc.tensor.matmul(
+                        out=y_bank[:, lh * BANK : (lh + 1) * BANK],
+                        lhsT=ident_bf[:],
+                        rhs=y_raw[:, images, :, :].rearrange("p n j w -> p n w j"),
+                        start=True,
+                        stop=True,
+                    )
+                nc.scalar.copy(out=y_grouped[:].rearrange("p l j -> p (l j)"), in_=y_bank[:])
 
             if with_y and k > 0:
                 regroup_y()
             for number, (a, b) in enumerate(loads):
                 g_raw = raws[number]
-                split = (b - a) * VECTOR_SHARE[0] // VECTOR_SHARE[1]
+                split = (b - a) * VECTOR_SHARE[0] // VECTOR_SHARE[1] // SHARE_STEP * SHARE_STEP
                 regroup(
                     nc.vector.tensor_copy,
                     g_grouped[:, a - col0 : a - col0 + split, :],
@@ -150,35 +156,35 @@ def tile_model_pa_k_kernel(tc, image, grad_output, grad_out, out):
                     scales=g_scales[:, w0:w1],
                     in_=g_grouped[:, w0:w1, :].rearrange("p w j -> p (w j)"),
                 )
-            for h in range(C_HALVES):
-                if not col0 <= h * HALF_COLS < col0 + ncols:
-                    continue
-                for lh in range(L_HALVES):
-                    places = slice(lh * P, (lh + 1) * P)
-                    for number in range(WINDOWS_PER_HALF):
-                        w0 = h * HALF_COLS - col0 + number * (HALF_COLS - BANK)
-                        nc.tensor.matmul_mx(
-                            out=t_acc[lh, h * WINDOWS_PER_HALF + number][:],
-                            lhsT=y_codes[:, places].bitcast(E4M3X4),
-                            lhsT_scale=y_scales[:, places],
-                            rhs=g_codes[:, w0 : w0 + BANK].bitcast(E5M2X4),
-                            rhs_scale=g_scales[:, w0 : w0 + BANK],
-                            start=(k == 0),
-                            stop=(k == PASSES - 1),
-                        )
-
-        def empty_banks(h):
-            copies = [nc.vector.tensor_copy, nc.scalar.copy]
-            for number in range(WINDOWS_PER_HALF):
-                s = h * WINDOWS_PER_HALF + number
-                first = number * (WINDOW_COLS - (HALF_COLS - BANK))
-                for lh in range(L_HALVES):
-                    copies[lh](
-                        out=t_sb[lh][:, :, s * WINDOW_C : (s + 1) * WINDOW_C],
-                        in_=t_acc[lh, s][:, first : first + WINDOW_COLS].rearrange(
-                            "p (c t) -> p t c", t=TAPS
-                        ),
+            for lh in range(L_HALVES):
+                places = slice(lh * P, (lh + 1) * P)
+                for w0 in range(0, ncols, BANK):
+                    nc.tensor.matmul_mx(
+                        out=t_acc[lh, (col0 + w0) // BANK][:],
+                        lhsT=y_codes[:, places].bitcast(E4M3X4),
+                        lhsT_scale=y_scales[:, places],
+                        rhs=g_codes[:, w0 : w0 + BANK].bitcast(E5M2X4),
+                        rhs_scale=g_scales[:, w0 : w0 + BANK],
+                        start=(k == 0),
+                        stop=(k == PASSES - 1),
                     )
+
+        def empty_banks(w):
+            copies = [nc.vector.tensor_copy, nc.scalar.copy]
+            first_whole = -(-w * BANK // TAPS)
+            end_whole = (w + 1) * BANK // TAPS
+            head = first_whole * TAPS - w * BANK
+            tail = (w + 1) * BANK - end_whole * TAPS
+            for lh in range(L_HALVES):
+                bank = t_acc[lh, w]
+                copies[lh](
+                    out=t_sb[lh][:, :, first_whole:end_whole],
+                    in_=bank[:, head : BANK - tail].rearrange("p (c t) -> p t c", t=TAPS),
+                )
+                if head:
+                    copies[lh](out=t_sb[lh][:, TAPS - head :, first_whole - 1], in_=bank[:, :head])
+                if tail:
+                    copies[lh](out=t_sb[lh][:, :tail, end_whole], in_=bank[:, BANK - tail :])
 
         def transpose_and_store(h):
             channels = slice(h * P, (h + 1) * P)
@@ -216,10 +222,12 @@ def tile_model_pa_k_kernel(tc, image, grad_output, grad_out, out):
         for i in range(len(plan) + 1):
             if i < len(plan):
                 load_and_regroup(plan[i])
-            if i == len(plan) - 1:
+            if i == len(plan) - 3:
                 empty_banks(0)
+            if i == len(plan) - 1:
+                empty_banks(1)
                 transpose_and_store(0)
             if i > 0:
                 quantise_and_multiply(plan[i - 1])
-        empty_banks(1)
+        empty_banks(2)
         transpose_and_store(1)

@@ -23,7 +23,7 @@ PACK = 4
 K_PASS = P * PACK
 PASSES = CO // K_PASS
 BANK = 512
-RUN = 4
+RUN = 8
 
 L_HALVES = L // P
 C_HALVES = CI // P

@@ -30,30 +30,29 @@ C_HALVES = CI // P
 
 WINDOWS = COLS // BANK
 
-VECTOR_SHARE = (49, 96)
+VECTOR_SHARE = (1, 2)
 SHARE_STEP = 2 * RUN
+
+QUANT_COLS = 512
+
+LOAD_AHEAD = 4
+IDENTITY_AHEAD = 3
+COPY_AHEAD = 2
 
 FLOPS = 2 * CO * COLS * L
 
 
 def units():
     plan = [
-        (0, 0, BANK, [(0, BANK // 2), (BANK // 2, BANK)], True),
-        (0, BANK, COLS - BANK, [(BANK, COLS)], False),
+        ((0,), 0, BANK, (0, BANK // 2, BANK)),
+        ((0,), BANK, COLS - BANK, (BANK, COLS)),
     ]
     for k in range(1, PASSES - 2):
-        plan.append((k, 0, COLS, [(0, COLS)], True))
+        plan.append(((k,), 0, COLS, (0, COLS)))
     for w in range(WINDOWS):
         for k in (PASSES - 2, PASSES - 1):
-            plan.append((k, w * BANK, BANK, [(w * BANK, (w + 1) * BANK)], w == 0))
+            plan.append(((k,), w * BANK, BANK, (w * BANK, (w + 1) * BANK)))
     return plan
-
-
-def regroup(copy, grouped, raw):
-    copy(
-        out=grouped.rearrange("p (q i) j -> p q j i", i=RUN),
-        in_=raw.rearrange("p j (q i) -> p q j i", i=RUN),
-    )
 
 
 def tile_model_pa_k_kernel(tc, image, grad_output, grad_out, out):
@@ -62,10 +61,24 @@ def tile_model_pa_k_kernel(tc, image, grad_output, grad_out, out):
     y_rows = grad_output.rearrange("n (k p j) h w -> k p n j (h w)", p=P, j=PACK)
     out_rows = out.rearrange("n c p q -> c n (p q)")
 
+    plan = units()
+    new_passes = []
+    seen = set()
+    for passes, col0, ncols, cuts in plan:
+        new_passes.append([k for k in passes if k not in seen])
+        for k in passes:
+            seen.add(k)
+    closes = {}
+    for i, (passes, col0, ncols, cuts) in enumerate(plan):
+        if PASSES - 1 in passes:
+            for w in range(col0 // BANK, (col0 + ncols) // BANK):
+                closes[w] = i
+
     with ExitStack() as ctx:
         const = ctx.enter_context(tc.tile_pool(name="const", bufs=1))
         raw_pool = ctx.enter_context(tc.tile_pool(name="raw", bufs=6))
-        grouped_pool = ctx.enter_context(tc.tile_pool(name="grouped", bufs=3))
+        g_grouped_pool = ctx.enter_context(tc.tile_pool(name="g_grouped", bufs=3))
+        y_grouped_pool = ctx.enter_context(tc.tile_pool(name="y_grouped", bufs=4))
         mx_pool = ctx.enter_context(tc.tile_pool(name="mx", bufs=3))
         psum = ctx.enter_context(tc.psum_pool(name="psum", bufs=1))
         stage = ctx.enter_context(tc.psum_pool(name="stage", bufs=2))
@@ -83,31 +96,37 @@ def tile_model_pa_k_kernel(tc, image, grad_output, grad_out, out):
 
         t_acc = {}
         for lh in range(L_HALVES):
-            for s in range(WINDOWS):
-                t_acc[lh, s] = psum.tile([P, BANK], F32, name="t_%d_%d" % (lh, s))
+            for w in range(WINDOWS):
+                t_acc[lh, w] = psum.tile([P, BANK], F32, name="t_%d_%d" % (lh, w))
 
+        g_raw_of = {}
+        y_raw_of = {}
+        y_bank_of = {}
         y_grouped_of = {}
         g_grouped_of = {}
         y_mx_of = {}
+        g_mx_of = {}
 
-        def load_and_regroup(unit):
-            k, col0, ncols, loads, with_y = unit
-            g_grouped = grouped_pool.tile([P, ncols, PACK], BF16, align_bytes=64, name="g_grouped")
-            g_grouped_of[k, col0] = g_grouped
-            raws = []
-            y_raw = None
-            for a, b in loads:
-                if with_y and y_raw is None and (k > 0 or raws):
-                    y_raw = raw_pool.tile([P, IMAGES, PACK, PLACES], BF16, name="y_raw")
-                    nc.sync.dma_start(out=y_raw[:], in_=y_rows[k])
-                g_raw = raw_pool.tile([P, PACK, b - a], BF16, name="g_raw")
-                nc.sync.dma_start(out=g_raw[:], in_=g_rows[k][:, :, a:b])
-                raws.append(g_raw)
+        def load(i):
+            passes, col0, ncols, cuts = plan[i]
+            g_raw_of[i] = []
+            for number in range(len(cuts) - 1):
+                if number == (1 if i == 0 else 0):
+                    for k in new_passes[i]:
+                        y_raw = raw_pool.tile([P, IMAGES, PACK, PLACES], BF16, name="y_raw")
+                        nc.sync.dma_start(out=y_raw[:], in_=y_rows[k])
+                        y_raw_of[k] = y_raw
+                a, b = cuts[number], cuts[number + 1]
+                g_raw = raw_pool.tile([P, len(passes), PACK, b - a], BF16, name="g_raw")
+                for kk, k in enumerate(passes):
+                    nc.sync.dma_start(out=g_raw[:, kk], in_=g_rows[k][:, :, a:b])
+                g_raw_of[i].append(g_raw)
 
-            def regroup_y():
-                y_grouped = grouped_pool.tile([P, L, PACK], BF16, align_bytes=64, name="y_grouped")
-                y_grouped_of[k] = y_grouped
+        def multiply_by_identity(i):
+            for k in new_passes[i]:
+                y_raw = y_raw_of.pop(k)
                 y_bank = stage.tile([P, L * PACK], BF16, name="y_bank")
+                y_bank_of[k] = y_bank
                 for lh in range(L_HALVES):
                     images = slice(lh * P // PLACES, (lh + 1) * P // PLACES)
                     nc.tensor.matmul(
@@ -117,57 +136,83 @@ def tile_model_pa_k_kernel(tc, image, grad_output, grad_out, out):
                         start=True,
                         stop=True,
                     )
-                nc.scalar.copy(out=y_grouped[:].rearrange("p l j -> p (l j)"), in_=y_bank[:])
 
-            if with_y and k > 0:
-                regroup_y()
-            for number, (a, b) in enumerate(loads):
-                g_raw = raws[number]
+        def copy_out_of_stage(i):
+            if not new_passes[i]:
+                return
+            y_grouped = y_grouped_pool.tile(
+                [P, len(new_passes[i]), L * PACK], BF16, align_bytes=64, name="y_grouped"
+            )
+            y_grouped_of[i] = y_grouped
+            for kk, k in enumerate(new_passes[i]):
+                nc.scalar.copy(out=y_grouped[:, kk, :], in_=y_bank_of.pop(k)[:])
+
+        def regroup(i):
+            passes, col0, ncols, cuts = plan[i]
+            g_grouped = g_grouped_pool.tile(
+                [P, len(passes), ncols, PACK], BF16, align_bytes=64, name="g_grouped"
+            )
+            g_grouped_of[i] = g_grouped
+            for number, g_raw in enumerate(g_raw_of.pop(i)):
+                a, b = cuts[number], cuts[number + 1]
                 split = (b - a) * VECTOR_SHARE[0] // VECTOR_SHARE[1] // SHARE_STEP * SHARE_STEP
-                regroup(
-                    nc.vector.tensor_copy,
-                    g_grouped[:, a - col0 : a - col0 + split, :],
-                    g_raw[:, :, :split],
-                )
-                regroup(nc.scalar.copy, g_grouped[:, a - col0 + split : b - col0, :], g_raw[:, :, split:])
-                if with_y and k == 0 and number == 0:
-                    regroup_y()
+                for kk in range(len(passes)):
+                    nc.vector.tensor_copy(
+                        out=g_grouped[:, kk, a - col0 : a - col0 + split, :].rearrange(
+                            "p (q i) j -> p q j i", i=RUN
+                        ),
+                        in_=g_raw[:, kk, :, :split].rearrange("p j (q i) -> p q j i", i=RUN),
+                    )
+                    nc.scalar.copy(
+                        out=g_grouped[:, kk, a - col0 + split : b - col0, :].rearrange(
+                            "p (q i) j -> p q j i", i=RUN
+                        ),
+                        in_=g_raw[:, kk, :, split:].rearrange("p j (q i) -> p q j i", i=RUN),
+                    )
 
-        def quantise_and_multiply(unit):
-            k, col0, ncols, loads, with_y = unit
-            if with_y:
-                y_grouped = y_grouped_of.pop(k)
-                y_codes = mx_pool.tile([P, L], U32, align_bytes=64, name="y_codes")
-                y_scales = mx_pool.tile([P, L], U8, align_bytes=64, name="y_scales")
-                y_mx_of[k] = (y_codes, y_scales)
+        def quantise(i):
+            passes, col0, ncols, cuts = plan[i]
+            if new_passes[i]:
+                width = len(new_passes[i]) * L
+                y_codes = mx_pool.tile([P, width], U32, align_bytes=64, name="y_codes")
+                y_scales = mx_pool.tile([P, width], U8, align_bytes=64, name="y_scales")
                 nc.vector.quantize_mx(
                     out=y_codes[:].bitcast(E4M3X4),
                     scales=y_scales[:],
-                    in_=y_grouped[:].rearrange("p l j -> p (l j)"),
+                    in_=y_grouped_of.pop(i)[:].rearrange("p k e -> p (k e)"),
                 )
-            y_codes, y_scales = y_mx_of[k]
-            g_grouped = g_grouped_of.pop((k, col0))
-            g_codes = mx_pool.tile([P, ncols], U32, align_bytes=64, name="g_codes")
-            g_scales = mx_pool.tile([P, ncols], U8, align_bytes=64, name="g_scales")
-            for w0 in range(0, ncols, BANK):
-                w1 = min(w0 + BANK, ncols)
+                for kk, k in enumerate(new_passes[i]):
+                    y_mx_of[k] = (y_codes, y_scales, kk * L)
+            width = len(passes) * ncols
+            g_grouped = g_grouped_of.pop(i)[:].rearrange("p k w j -> p (k w j)")
+            g_codes = mx_pool.tile([P, width], U32, align_bytes=64, name="g_codes")
+            g_scales = mx_pool.tile([P, width], U8, align_bytes=64, name="g_scales")
+            g_mx_of[i] = (g_codes, g_scales)
+            for w0 in range(0, width, QUANT_COLS):
+                w1 = min(w0 + QUANT_COLS, width)
                 nc.vector.quantize_mx(
                     out=g_codes[:, w0:w1].bitcast(E5M2X4),
                     scales=g_scales[:, w0:w1],
-                    in_=g_grouped[:, w0:w1, :].rearrange("p w j -> p (w j)"),
+                    in_=g_grouped[:, w0 * PACK : w1 * PACK],
                 )
-            for lh in range(L_HALVES):
-                places = slice(lh * P, (lh + 1) * P)
-                for w0 in range(0, ncols, BANK):
-                    nc.tensor.matmul_mx(
-                        out=t_acc[lh, (col0 + w0) // BANK][:],
-                        lhsT=y_codes[:, places].bitcast(E4M3X4),
-                        lhsT_scale=y_scales[:, places],
-                        rhs=g_codes[:, w0 : w0 + BANK].bitcast(E5M2X4),
-                        rhs_scale=g_scales[:, w0 : w0 + BANK],
-                        start=(k == 0),
-                        stop=(k == PASSES - 1),
-                    )
+
+        def multiply(i):
+            passes, col0, ncols, cuts = plan[i]
+            g_codes, g_scales = g_mx_of.pop(i)
+            for kk, k in enumerate(passes):
+                y_codes, y_scales, y0 = y_mx_of[k]
+                for lh in range(L_HALVES):
+                    places = slice(y0 + lh * P, y0 + (lh + 1) * P)
+                    for w0 in range(kk * ncols, (kk + 1) * ncols, BANK):
+                        nc.tensor.matmul_mx(
+                            out=t_acc[lh, (col0 + w0 - kk * ncols) // BANK][:],
+                            lhsT=y_codes[:, places].bitcast(E4M3X4),
+                            lhsT_scale=y_scales[:, places],
+                            rhs=g_codes[:, w0 : w0 + BANK].bitcast(E5M2X4),
+                            rhs_scale=g_scales[:, w0 : w0 + BANK],
+                            start=(k == 0),
+                            stop=(k == PASSES - 1),
+                        )
 
         def empty_banks(w):
             copies = [nc.vector.tensor_copy, nc.scalar.copy]
@@ -218,16 +263,35 @@ def tile_model_pa_k_kernel(tc, image, grad_output, grad_out, out):
                 out=out_rows[channels], in_=out_sb[h][:].rearrange("c n p q -> c n (p q)")
             )
 
-        plan = units()
-        for i in range(len(plan) + 1):
-            if i < len(plan):
-                load_and_regroup(plan[i])
-            if i == len(plan) - 3:
-                empty_banks(0)
-            if i == len(plan) - 1:
-                empty_banks(1)
-                transpose_and_store(0)
-            if i > 0:
-                quantise_and_multiply(plan[i - 1])
-        empty_banks(2)
-        transpose_and_store(1)
+        def in_plan(i):
+            return 0 <= i < len(plan)
+
+        written = {"identity": 0, "copy": 0}
+
+        def grad_output_ahead(t):
+            for i in range(written["copy"], min(t + COPY_AHEAD, len(plan) - 1) + 1):
+                if written["identity"] == i:
+                    multiply_by_identity(i)
+                    written["identity"] = i + 1
+                copy_out_of_stage(i)
+                written["copy"] = i + 1
+            for i in range(written["identity"], min(t + IDENTITY_AHEAD, len(plan) - 1) + 1):
+                multiply_by_identity(i)
+                written["identity"] = i + 1
+
+        for i in range(LOAD_AHEAD):
+            load(i)
+        for t in range(len(plan) + 2):
+            if in_plan(t + LOAD_AHEAD):
+                load(t + LOAD_AHEAD)
+            if in_plan(t):
+                regroup(t)
+                grad_output_ahead(t)
+            for w in range(WINDOWS):
+                if closes[w] == t - 2:
+                    empty_banks(w)
+                    if w > 0:
+                        transpose_and_store(w - 1)
+            if in_plan(t - 1):
+                quantise(t - 1)
+                multiply(t - 1)

@@ -30,7 +30,7 @@ C_HALVES = CI // P
 
 WINDOWS = COLS // BANK
 
-VECTOR_SHARE = (1, 2)
+VECTOR_SHARE = (49, 96)
 SHARE_STEP = 2 * RUN
 
 QUANT_COLS = 512
@@ -38,6 +38,8 @@ QUANT_COLS = 512
 LOAD_AHEAD = 4
 IDENTITY_AHEAD = 3
 COPY_AHEAD = 2
+
+SPLIT_PASSES = 3
 
 FLOPS = 2 * CO * COLS * L
 
@@ -47,11 +49,11 @@ def units():
         ((0,), 0, BANK, (0, BANK // 2, BANK)),
         ((0,), BANK, COLS - BANK, (BANK, COLS)),
     ]
-    for k in range(1, PASSES - 2):
+    for k in range(1, PASSES - SPLIT_PASSES):
         plan.append(((k,), 0, COLS, (0, COLS)))
-    for w in range(WINDOWS):
-        for k in (PASSES - 2, PASSES - 1):
-            plan.append(((k,), w * BANK, BANK, (w * BANK, (w + 1) * BANK)))
+    for a, b in ((0, COLS - BANK), (COLS - BANK, COLS)):
+        for k in range(PASSES - SPLIT_PASSES, PASSES):
+            plan.append(((k,), a, b - a, (a, b)))
     return plan
 
 
@@ -231,9 +233,10 @@ def tile_model_pa_k_kernel(tc, image, grad_output, grad_out, out):
                 if tail:
                     copies[lh](out=t_sb[lh][:, :tail, end_whole], in_=bank[:, BANK - tail :])
 
-        def transpose_and_store(h):
+        sums = {}
+
+        def transpose(h):
             channels = slice(h * P, (h + 1) * P)
-            sums = {}
             for kw in reversed(range(KW)):
                 bank = psum.tile([P, BANK], F32, name="sums_%d_%d" % (h, kw), tag="t_%d_%d" % (kw, h))
                 nc.tensor.matmul(out=bank[:], lhsT=zeros[:, :P], rhs=zeros[:], start=True, stop=False)
@@ -249,14 +252,17 @@ def tile_model_pa_k_kernel(tc, image, grad_output, grad_out, out):
                             start=False,
                             stop=(lh == L_HALVES - 1 and kh == KH - 1),
                         )
-                sums[kw] = bank[:, : IMAGES * H * WO].rearrange(
+                sums[h, kw] = bank[:, : IMAGES * H * WO].rearrange(
                     "c (n p j) -> c n p j", n=IMAGES, p=H
                 )
-            nc.scalar.copy(out=out_sb[h][:, :, :, 1 : 1 + WO], in_=sums[1])
+
+        def add_and_store(h):
+            channels = slice(h * P, (h + 1) * P)
+            nc.scalar.copy(out=out_sb[h][:, :, :, 1 : 1 + WO], in_=sums[h, 1])
             nc.vector.tensor_tensor(
                 out=out_sb[h][:, :, :, 0:WO],
                 in0=out_sb[h][:, :, :, 0:WO],
-                in1=sums[0],
+                in1=sums[h, 0],
                 op=mybir.AluOpType.add,
             )
             nc.sync.dma_start(
@@ -269,19 +275,19 @@ def tile_model_pa_k_kernel(tc, image, grad_output, grad_out, out):
         written = {"identity": 0, "copy": 0}
 
         def grad_output_ahead(t):
-            for i in range(written["copy"], min(t + COPY_AHEAD, len(plan) - 1) + 1):
+            for i in range(written["copy"], min(t + min(t, COPY_AHEAD), len(plan) - 1) + 1):
                 if written["identity"] == i:
                     multiply_by_identity(i)
                     written["identity"] = i + 1
                 copy_out_of_stage(i)
                 written["copy"] = i + 1
-            for i in range(written["identity"], min(t + IDENTITY_AHEAD, len(plan) - 1) + 1):
+            for i in range(written["identity"], min(t + min(t + 1, IDENTITY_AHEAD), len(plan) - 1) + 1):
                 multiply_by_identity(i)
                 written["identity"] = i + 1
 
         for i in range(LOAD_AHEAD):
             load(i)
-        for t in range(len(plan) + 2):
+        for t in range(len(plan) + 3):
             if in_plan(t + LOAD_AHEAD):
                 load(t + LOAD_AHEAD)
             if in_plan(t):
@@ -291,7 +297,10 @@ def tile_model_pa_k_kernel(tc, image, grad_output, grad_out, out):
                 if closes[w] == t - 2:
                     empty_banks(w)
                     if w > 0:
-                        transpose_and_store(w - 1)
+                        transpose(w - 1)
             if in_plan(t - 1):
                 quantise(t - 1)
                 multiply(t - 1)
+            for w in range(1, WINDOWS):
+                if closes[w] == t - 3:
+                    add_and_store(w - 1)

@@ -45,11 +45,8 @@ FLOPS = 2 * CO * COLS * L
 
 
 def units():
-    plan = [
-        ((0,), 0, BANK, (0, BANK // 2, BANK)),
-        ((0,), BANK, COLS - BANK, (BANK, COLS)),
-    ]
-    for k in range(1, PASSES - SPLIT_PASSES):
+    plan = []
+    for k in range(PASSES - SPLIT_PASSES):
         plan.append(((k,), 0, COLS, (0, COLS)))
     for a, b in ((0, COLS - BANK), (COLS - BANK, COLS)):
         for k in range(PASSES - SPLIT_PASSES, PASSES):
@@ -113,7 +110,7 @@ def tile_model_pa_k_kernel(tc, image, grad_output, grad_out, out):
             passes, col0, ncols, cuts = plan[i]
             g_raw_of[i] = []
             for number in range(len(cuts) - 1):
-                if number == (1 if i == 0 else 0):
+                if number == 0:
                     for k in new_passes[i]:
                         y_raw = raw_pool.tile([P, IMAGES, PACK, PLACES], BF16, name="y_raw")
                         nc.sync.dma_start(out=y_raw[:], in_=y_rows[k])

from contextlib import ExitStack

import concourse.mybir as mybir
from concourse.masks import make_identity

BF16 = mybir.dt.bfloat16
F32 = mybir.dt.float32
U32 = mybir.dt.uint32
U8 = mybir.dt.uint8
E4M3X4 = mybir.dt.float8_e4m3fn_x4
E5M2X4 = mybir.dt.float8_e5m2_x4

IMAGES, CI, CO = 4, 256, 8192
H, W, KH, KW = 10, 9, 3, 2
HO, WO = H - KH + 1, W - KW + 1
TAPS = KH * KW
PLACES = HO * WO
L = IMAGES * PLACES
COLS = CI * TAPS

P = 128
PACK = 4
K_PASS = P * PACK
PASSES = CO // K_PASS
BANK = 512
RUN = 8

L_HALVES = L // P
C_HALVES = CI // P

WINDOWS = COLS // BANK

VECTOR_SHARE = (49, 96)
SHARE_STEP = 2 * RUN

QUANT_COLS = 512

LOAD_AHEAD = 4
IDENTITY_AHEAD = 3
COPY_AHEAD = 2

SPLIT_PASSES = 3

FLOPS = 2 * CO * COLS * L


def units():
    plan = []
    for k in range(PASSES - SPLIT_PASSES):
        plan.append(((k,), 0, COLS, (0, COLS)))
    for a, b in ((0, COLS - BANK), (COLS - BANK, COLS)):
        for k in range(PASSES - SPLIT_PASSES, PASSES):
            plan.append(((k,), a, b - a, (a, b)))
    return plan


def tile_model_pa_k_kernel(tc, image, grad_output, grad_out, out):
    nc = tc.nc
    g_rows = grad_out.rearrange("(k p j) c kh kw -> k p j (c kh kw)", p=P, j=PACK)
    y_rows = grad_output.rearrange("n (k p j) h w -> k p n j (h w)", p=P, j=PACK)
    out_rows = out.rearrange("n c p q -> c n (p q)")

    plan = units()
    new_passes = []
    seen = set()
    for passes, col0, ncols, cuts in plan:
        new_passes.append([k for k in passes if k not in seen])
        for k in passes:
            seen.add(k)
    closes = {}
    for i, (passes, col0, ncols, cuts) in enumerate(plan):
        if PASSES - 1 in passes:
            for w in range(col0 // BANK, (col0 + ncols) // BANK):
                closes[w] = i

    with ExitStack() as ctx:
        const = ctx.enter_context(tc.tile_pool(name="const", bufs=1))
        raw_pool = ctx.enter_context(tc.tile_pool(name="raw", bufs=6))
        g_grouped_pool = ctx.enter_context(tc.tile_pool(name="g_grouped", bufs=3))
        y_grouped_pool = ctx.enter_context(tc.tile_pool(name="y_grouped", bufs=4))
        mx_pool = ctx.enter_context(tc.tile_pool(name="mx", bufs=3))
        psum = ctx.enter_context(tc.psum_pool(name="psum", bufs=1))
        stage = ctx.enter_context(tc.psum_pool(name="stage", bufs=2))

        ident = const.tile([P, P], F32)
        make_identity(nc, ident[:])
        ident_bf = const.tile([P, P], BF16)
        make_identity(nc, ident_bf[:])
        zeros = const.tile([P, BANK], BF16)
        nc.vector.memset(zeros[:], 0.0)
        out_sb = [const.tile([P, IMAGES, H, W], F32, name="out_sb%d" % h) for h in range(C_HALVES)]
        for h in range(C_HALVES):
            nc.vector.memset(out_sb[h][:], 0.0)
        t_sb = [const.tile([P, TAPS, CI], F32, name="t_sb%d" % lh) for lh in range(L_HALVES)]

        t_acc = {}
        for lh in range(L_HALVES):
            for w in range(WINDOWS):
                t_acc[lh, w] = psum.tile([P, BANK], F32, name="t_%d_%d" % (lh, w))

        g_raw_of = {}
        y_raw_of = {}
        y_bank_of = {}
        y_grouped_of = {}
        g_grouped_of = {}
        y_mx_of = {}
        g_mx_of = {}

        def load(i):
            passes, col0, ncols, cuts = plan[i]
            g_raw_of[i] = []
            for number in range(len(cuts) - 1):
                if number == 0:
                    for k in new_passes[i]:
                        y_raw = raw_pool.tile([P, IMAGES, PACK, PLACES], BF16, name="y_raw")
                        nc.sync.dma_start(out=y_raw[:], in_=y_rows[k])
                        y_raw_of[k] = y_raw
                a, b = cuts[number], cuts[number + 1]
                g_raw = raw_pool.tile([P, len(passes), PACK, b - a], BF16, name="g_raw")
                for kk, k in enumerate(passes):
                    nc.sync.dma_start(out=g_raw[:, kk], in_=g_rows[k][:, :, a:b])
                g_raw_of[i].append(g_raw)

        def multiply_by_identity(i):
            for k in new_passes[i]:
                y_raw = y_raw_of.pop(k)
                y_bank = stage.tile([P, L * PACK], BF16, name="y_bank")
                y_bank_of[k] = y_bank
                for lh in range(L_HALVES):
                    images = slice(lh * P // PLACES, (lh + 1) * P // PLACES)
                    nc.tensor.matmul(
                        out=y_bank[:, lh * BANK : (lh + 1) * BANK],
                        lhsT=ident_bf[:],
                        rhs=y_raw[:, images, :, :].rearrange("p n j w -> p n w j"),
                        start=True,
                        stop=True,
                    )

        def copy_out_of_stage(i):
            if not new_passes[i]:
                return
            y_grouped = y_grouped_pool.tile(
                [P, len(new_passes[i]), L * PACK], BF16, align_bytes=64, name="y_grouped"
            )
            y_grouped_of[i] = y_grouped
            for kk, k in enumerate(new_passes[i]):
                nc.scalar.copy(out=y_grouped[:, kk, :], in_=y_bank_of.pop(k)[:])

        def regroup(i):
            passes, col0, ncols, cuts = plan[i]
            g_grouped = g_grouped_pool.tile(
                [P, len(passes), ncols, PACK], BF16, align_bytes=64, name="g_grouped"
            )
            g_grouped_of[i] = g_grouped
            for number, g_raw in enumerate(g_raw_of.pop(i)):
                a, b = cuts[number], cuts[number + 1]
                split = (b - a) * VECTOR_SHARE[0] // VECTOR_SHARE[1] // SHARE_STEP * SHARE_STEP
                for kk in range(len(passes)):
                    nc.vector.tensor_copy(
                        out=g_grouped[:, kk, a - col0 : a - col0 + split, :].rearrange(
                            "p (q i) j -> p q j i", i=RUN
                        ),
                        in_=g_raw[:, kk, :, :split].rearrange("p j (q i) -> p q j i", i=RUN),
                    )
                    nc.scalar.copy(
                        out=g_grouped[:, kk, a - col0 + split : b - col0, :].rearrange(
                            "p (q i) j -> p q j i", i=RUN
                        ),
                        in_=g_raw[:, kk, :, split:].rearrange("p j (q i) -> p q j i", i=RUN),
                    )

        def quantise(i):
            passes, col0, ncols, cuts = plan[i]
            if new_passes[i]:
                width = len(new_passes[i]) * L
                y_codes = mx_pool.tile([P, width], U32, align_bytes=64, name="y_codes")
                y_scales = mx_pool.tile([P, width], U8, align_bytes=64, name="y_scales")
                nc.vector.quantize_mx(
                    out=y_codes[:].bitcast(E4M3X4),
                    scales=y_scales[:],
                    in_=y_grouped_of.pop(i)[:].rearrange("p k e -> p (k e)"),
                )
                for kk, k in enumerate(new_passes[i]):
                    y_mx_of[k] = (y_codes, y_scales, kk * L)
            width = len(passes) * ncols
            g_grouped = g_grouped_of.pop(i)[:].rearrange("p k w j -> p (k w j)")
            g_codes = mx_pool.tile([P, width], U32, align_bytes=64, name="g_codes")
            g_scales = mx_pool.tile([P, width], U8, align_bytes=64, name="g_scales")
            g_mx_of[i] = (g_codes, g_scales)
            for w0 in range(0, width, QUANT_COLS):
                w1 = min(w0 + QUANT_COLS, width)
                nc.vector.quantize_mx(
                    out=g_codes[:, w0:w1].bitcast(E5M2X4),
                    scales=g_scales[:, w0:w1],
                    in_=g_grouped[:, w0 * PACK : w1 * PACK],
                )

        def multiply(i):
            passes, col0, ncols, cuts = plan[i]
            g_codes, g_scales = g_mx_of.pop(i)
            for kk, k in enumerate(passes):
                y_codes, y_scales, y0 = y_mx_of[k]
                for lh in range(L_HALVES):
                    places = slice(y0 + lh * P, y0 + (lh + 1) * P)
                    for w0 in range(kk * ncols, (kk + 1) * ncols, BANK):
                        nc.tensor.matmul_mx(
                            out=t_acc[lh, (col0 + w0 - kk * ncols) // BANK][:],
                            lhsT=y_codes[:, places].bitcast(E4M3X4),
                            lhsT_scale=y_scales[:, places],
                            rhs=g_codes[:, w0 : w0 + BANK].bitcast(E5M2X4),
                            rhs_scale=g_scales[:, w0 : w0 + BANK],
                            start=(k == 0),
                            stop=(k == PASSES - 1),
                        )

        def empty_banks(w):
            copies = [nc.vector.tensor_copy, nc.scalar.copy]
            first_whole = -(-w * BANK // TAPS)
            end_whole = (w + 1) * BANK // TAPS
            head = first_whole * TAPS - w * BANK
            tail = (w + 1) * BANK - end_whole * TAPS
            for lh in range(L_HALVES):
                bank = t_acc[lh, w]
                copies[lh](
                    out=t_sb[lh][:, :, first_whole:end_whole],
                    in_=bank[:, head : BANK - tail].rearrange("p (c t) -> p t c", t=TAPS),
                )
                if head:
                    copies[lh](out=t_sb[lh][:, TAPS - head :, first_whole - 1], in_=bank[:, :head])
                if tail:
                    copies[lh](out=t_sb[lh][:, :tail, end_whole], in_=bank[:, BANK - tail :])

        sums = {}

        def transpose(h):
            channels = slice(h * P, (h + 1) * P)
            for kw in reversed(range(KW)):
                bank = psum.tile([P, BANK], F32, name="sums_%d_%d" % (h, kw), tag="t_%d_%d" % (kw, h))
                nc.tensor.matmul(out=bank[:], lhsT=zeros[:, :P], rhs=zeros[:], start=True, stop=False)
                rows = bank[:, : IMAGES * H * WO].rearrange("c (n r) -> c n r", n=IMAGES)
                for lh in range(L_HALVES):
                    images = slice(lh * P // PLACES, (lh + 1) * P // PLACES)
                    for kh in range(KH):
                        nc.tensor.matmul(
                            out=rows[:, images, kh * WO : kh * WO + PLACES],
                            lhsT=t_sb[lh][:, kh * KW + kw, channels],
                            rhs=ident[:],
                            is_transpose=True,
                            start=False,
                            stop=(lh == L_HALVES - 1 and kh == KH - 1),
                        )
                sums[h, kw] = bank[:, : IMAGES * H * WO].rearrange(
                    "c (n p j) -> c n p j", n=IMAGES, p=H
                )

        def add_and_store(h):
            channels = slice(h * P, (h + 1) * P)
            nc.scalar.copy(out=out_sb[h][:, :, :, 1 : 1 + WO], in_=sums[h, 1])
            nc.vector.tensor_tensor(
                out=out_sb[h][:, :, :, 0:WO],
                in0=out_sb[h][:, :, :, 0:WO],
                in1=sums[h, 0],
                op=mybir.AluOpType.add,
            )
            nc.sync.dma_start(
                out=out_rows[channels], in_=out_sb[h][:].rearrange("c n p q -> c n (p q)")
            )

        def in_plan(i):
            return 0 <= i < len(plan)

        written = {"identity": 0, "copy": 0}

        def grad_output_ahead(t):
            for i in range(written["copy"], min(t + min(t, COPY_AHEAD), len(plan) - 1) + 1):
                if written["identity"] == i:
                    multiply_by_identity(i)
                    written["identity"] = i + 1
                copy_out_of_stage(i)
                written["copy"] = i + 1
            for i in range(written["identity"], min(t + min(t + 1, IDENTITY_AHEAD), len(plan) - 1) + 1):
                multiply_by_identity(i)
                written["identity"] = i + 1

        for i in range(LOAD_AHEAD):
            load(i)
        for t in range(len(plan) + 3):
            if in_plan(t + LOAD_AHEAD):
                load(t + LOAD_AHEAD)
            if in_plan(t):
                regroup(t)
                grad_output_ahead(t)
            for w in range(WINDOWS):
                if closes[w] == t - 2:
                    empty_banks(w)
                    if w > 0:
                        transpose(w - 1)
            if in_plan(t - 1):
                quantise(t - 1)
                multiply(t - 1)
            for w in range(1, WINDOWS):
                if closes[w] == t - 3:
                    add_and_store(w - 1)
